import numpy as np
import ml_dtypes


def mxq(x, axis, fmt="e4m3"):
    dtype, down = {"e4m3": (ml_dtypes.float8_e4m3fn, 7), "e5m2": (ml_dtypes.float8_e5m2, 14)}[fmt]
    v = np.moveaxis(np.asarray(x, np.float32).astype(ml_dtypes.bfloat16).astype(np.float64), axis, -1)
    blocks = v.reshape(v.shape[:-1] + (-1, 32))
    amax = np.abs(blocks).max(-1, keepdims=True)
    byte = np.maximum(np.where(amax > 0, np.frexp(amax)[1] - 1 + 127, 0) - down, 1)
    scale = np.exp2(byte - 127.0)
    codes = (blocks / scale).astype(np.float32).astype(dtype).astype(np.float64)
    return np.moveaxis((codes * scale).reshape(v.shape), -1, axis)


WIDE = False


def mx_kscale(k):
    if not WIDE:
        return np.ones(k)
    levels = np.array([10, -10, 5, -5, 0])
    a = np.random.permutation(np.resize(levels, k // 512 * 4)).reshape(k // 512, 4)
    idx = np.arange(k)
    return np.exp2(a[idx // 512, idx % 128 // 32])


BF16 = ml_dtypes.bfloat16


def bf(x):
    return np.asarray(x, np.float32).astype(BF16)


def f64(x):
    return np.asarray(x).astype(np.float64)


E2M1 = np.array([0.0, 0.5, 1.0, 1.5, 2.0, 3.0, 4.0, 6.0, -0.0, -0.5, -1.0, -1.5, -2.0, -3.0, -4.0, -6.0])


def pack_weight(w, fmt):
    k, n = w.shape
    w = f64(bf(w)).reshape(k // 32, 32, n)
    amax = np.abs(w).max(1)
    if fmt == "e4m3":
        byte = np.frexp(amax)[1] - 1 + 127 - 7
    else:
        mant, ex = np.frexp(amax / 6.0)
        byte = np.where(mant > 0.5, ex, ex - 1) + 127
    byte = np.clip(np.where(amax > 0, byte, 1), 1, 254)
    scaled = (w * np.exp2(127.0 - byte)[:, None, :]).reshape(k, n).astype(np.float32)
    by_word = np.ascontiguousarray(scaled.reshape(k // 512, 128, 4, n).transpose(0, 1, 3, 2))
    if fmt == "e4m3":
        words = by_word.astype(ml_dtypes.float8_e4m3fn).view(np.uint8)
    else:
        c = by_word.astype(ml_dtypes.float4_e2m1fn).view(np.uint8) & 0xF
        words = c[..., 0::2] | (c[..., 1::2] << 4)
    return np.ascontiguousarray(words), np.ascontiguousarray(byte.astype(np.uint8).reshape(k // 512, 16, n))


def unpack_weight(words, scales, fmt):
    g, p, n, _ = words.shape
    if fmt == "e4m3":
        vals = np.ascontiguousarray(words).view(ml_dtypes.float8_e4m3fn).astype(np.float64)
    else:
        nib = np.empty((g, p, n, 4), np.uint8)
        nib[..., 0::2] = words & 0xF
        nib[..., 1::2] = words >> 4
        vals = E2M1[nib]
    vals = vals * np.repeat(np.exp2(scales.astype(np.float64) - 127.0), 8, axis=1)[..., None]
    return vals.transpose(0, 1, 3, 2).reshape(g * 512, n)


B, K, N = 16384, 512, 256


def setup_inputs():
    s = mx_kscale(K)
    x = bf(np.random.standard_normal((B, K)) * s)
    dft_real = np.random.standard_normal((N, K)) / np.sqrt(K) / s[None, :]
    dft_imag = np.random.standard_normal((N, K)) / np.sqrt(K) / s[None, :]
    dft_real_words, dft_real_scales = pack_weight(dft_real.T, "e4m3")
    dft_imag_words, dft_imag_scales = pack_weight(dft_imag.T, "e4m3")
    return {"x": x,
            "dft_real_words": dft_real_words,
            "dft_real_scales": dft_real_scales,
            "dft_imag_words": dft_imag_words,
            "dft_imag_scales": dft_imag_scales}


def reference(x, dft_real_words, dft_real_scales, dft_imag_words, dft_imag_scales):
    xq = mxq(f64(x), 1, "e4m3")
    rxs = xq @ unpack_weight(dft_real_words, dft_real_scales, "e4m3")
    ixs = xq @ unpack_weight(dft_imag_words, dft_imag_scales, "e4m3")
    mag = np.log(rxs * rxs + ixs * ixs)
    return mag

@@ -1,0 +1,165 @@
+from contextlib import ExitStack
+
+import concourse.mybir as mybir
+from concourse.masks import make_identity
+
+F32 = mybir.dt.float32
+BF16 = mybir.dt.bfloat16
+I32 = mybir.dt.int32
+U32 = mybir.dt.uint32
+U8 = mybir.dt.uint8
+FP8X4 = mybir.dt.float8_e4m3fn_x4
+ACT = mybir.ActivationFunctionType
+ALU = mybir.AluOpType
+
+P = 128
+PACK = 4
+ROWS, K, N = 16384, 512, 256
+assert K == P * PACK
+
+TILES = 4
+GROUP_ROWS = TILES * P
+N_GROUPS = ROWS // GROUP_ROWS
+WORDS = K // 2
+LOADS_AHEAD = 7
+
+FLOPS = 2 * ROWS * K * 2 * N
+
+
+def tile_dft_kernel(
+    tc, x, dft_real_words, dft_real_scales, dft_imag_words, dft_imag_scales, out
+):
+    nc = tc.nc
+    x_groups = x.rearrange("(g p j) k -> g p j k", p=P, j=TILES)
+    out_groups = out.rearrange("(g p j) n -> g p j n", p=P, j=TILES)
+
+    with ExitStack() as ctx:
+        ctx.enter_context(tc.manual_schedule())
+        consts = ctx.enter_context(tc.tile_pool(name="consts", bufs=1))
+        x_pool = ctx.enter_context(tc.tile_pool(name="x", bufs=LOADS_AHEAD + 1))
+        grouped_pool = ctx.enter_context(tc.tile_pool(name="grouped", bufs=2))
+        codes_pool = ctx.enter_context(tc.tile_pool(name="codes", bufs=2))
+        squares_pool = ctx.enter_context(tc.tile_pool(name="squares", bufs=3))
+        out_pool = ctx.enter_context(tc.tile_pool(name="out", bufs=3))
+        turned_pool = ctx.enter_context(tc.psum_pool(name="turned", bufs=4))
+        product_pool = ctx.enter_context(tc.psum_pool(name="product", bufs=4))
+
+        x_tiles = {}
+        turned_tiles = {}
+        grouped_tiles = {}
+        code_tiles = {}
+        square_tiles = {}
+        out_tiles = {}
+
+        def load_x(g):
+            x_sb = x_pool.tile([P, TILES, K], BF16)
+            nc.sync.dma_start(out=x_sb[:], in_=x_groups[g])
+            x_tiles[g] = x_sb
+
+        def transpose_group(g):
+            x_words = x_tiles[g][:].bitcast(F32)
+            turned_tiles[g] = []
+            for half in range(TILES // 2):
+                turned = turned_pool.tile([P, 2, 2, P], F32)
+                for j in range(2):
+                    for u in range(2):
+                        nc.tensor.transpose(
+                            out=turned[:, j, u, :],
+                            in_=x_words[:, 2 * half + j, u:WORDS:2],
+                            identity=identity[:],
+                        )
+                turned_tiles[g].append(turned)
+
+        def regroup(g):
+            grouped = grouped_pool.tile([P, TILES, P, PACK], BF16, align_bytes=64)
+            grouped_words = grouped[:].bitcast(F32)
+            for half in range(TILES // 2):
+                nc.vector.tensor_copy(
+                    out=grouped_words[:, 2 * half : 2 * half + 2, :, :],
+                    in_=turned_tiles[g][half][:].rearrange("p j u r -> p j r u"),
+                )
+            grouped_tiles[g] = grouped
+
+        def quantise(g):
+            x_codes = codes_pool.tile([P, TILES * P], U32, align_bytes=64)
+            x_scales = codes_pool.tile([P, TILES * P], U8, align_bytes=64)
+            nc.vector.quantize_mx(
+                out=x_codes[:].bitcast(FP8X4),
+                scales=x_scales[:],
+                in_=grouped_tiles[g][:].rearrange("p j r t -> p (j r t)"),
+            )
+            code_tiles[g] = (x_codes, x_scales)
+
+        def project_and_square(g):
+            x_codes, x_scales = code_tiles[g]
+            squares = squares_pool.tile([P, TILES, 2 * N], F32)
+            for j in range(TILES):
+                rows = slice(j * P, (j + 1) * P)
+                product = product_pool.tile([P, 2 * N], F32)
+                nc.tensor.matmul_mx(
+                    out=product[:],
+                    lhsT=x_codes[:, rows].bitcast(FP8X4),
+                    lhsT_scale=x_scales[:, rows],
+                    rhs=w_codes[:].bitcast(FP8X4),
+                    rhs_scale=w_scales[:],
+                    start=True,
+                    stop=True,
+                )
+                nc.scalar.activation(out=squares[:, j, :], in_=product[:], func=ACT.Square)
+            square_tiles[g] = squares
+
+        def add_squares(g):
+            squares = square_tiles[g]
+            power = out_pool.tile([P, TILES, N], F32)
+            nc.vector.tensor_tensor(
+                out=power[:], in0=squares[:, :, 0:N], in1=squares[:, :, N : 2 * N], op=ALU.add
+            )
+            out_tiles[g] = power
+
+        def log_and_store(g):
+            power = out_tiles[g]
+            nc.scalar.activation(out=power[:], in_=power[:], func=ACT.Ln)
+            nc.sync.dma_start(out=out_groups[g], in_=power[:])
+
+        w_scales = consts.tile([P, 2 * N], U8, align_bytes=64)
+        nc.vector.memset(w_scales[:].bitcast(I32), 0)
+        one = consts.tile([P, 1], F32)
+        nc.vector.memset(one[:], 1.0)
+        nc.scalar.activation(out=one[:], in_=one[:], func=ACT.Ln)
+        identity = consts.tile([P, P], F32)
+        make_identity(nc, identity[:])
+
+        load_x(0)
+        w_codes = consts.tile([P, 2 * N], U32, align_bytes=64)
+        for m, (words, scales) in enumerate(
+            ((dft_real_words, dft_real_scales), (dft_imag_words, dft_imag_scales))
+        ):
+            cols = slice(m * N, (m + 1) * N)
+            nc.sync.dma_start(
+                out=w_codes[:, cols].bitcast(I32),
+                in_=words.rearrange("g p n t -> (g p) (n t)").bitcast(I32),
+            )
+            scale_rows = scales.rearrange("g q n -> (g q) n")
+            for quadrant in range(4):
+                nc.sync.dma_start(
+                    out=w_scales[32 * quadrant : 32 * quadrant + 4, cols].bitcast(I32),
+                    in_=scale_rows[4 * quadrant : 4 * quadrant + 4, :].bitcast(I32),
+                )
+        for g in range(1, LOADS_AHEAD):
+            load_x(g)
+
+        for step in range(N_GROUPS + 2):
+            turning, projecting, finishing = step, step - 1, step - 2
+            if turning + LOADS_AHEAD < N_GROUPS:
+                load_x(turning + LOADS_AHEAD)
+            if turning < N_GROUPS:
+                transpose_group(turning)
+                regroup(turning)
+            if 0 <= projecting < N_GROUPS:
+                project_and_square(projecting)
+            if finishing >= 0:
+                add_squares(finishing)
+            if turning < N_GROUPS:
+                quantise(turning)
+            if finishing >= 0:
+                log_and_store(finishing)

@@ -39,8 +39,9 @@ def tile_dft_kernel(
         x_pool = ctx.enter_context(tc.tile_pool(name="x", bufs=LOADS_AHEAD + 1))
         grouped_pool = ctx.enter_context(tc.tile_pool(name="grouped", bufs=2))
         codes_pool = ctx.enter_context(tc.tile_pool(name="codes", bufs=2))
+        copy_pool = ctx.enter_context(tc.tile_pool(name="copy", bufs=2))
         squares_pool = ctx.enter_context(tc.tile_pool(name="squares", bufs=3))
-        out_pool = ctx.enter_context(tc.tile_pool(name="out", bufs=3))
+        out_pool = ctx.enter_context(tc.tile_pool(name="out", bufs=4))
         turned_pool = ctx.enter_context(tc.psum_pool(name="turned", bufs=4))
         product_pool = ctx.enter_context(tc.psum_pool(name="product", bufs=4))
 
@@ -105,13 +106,22 @@ def tile_dft_kernel(
                     start=True,
                     stop=True,
                 )
-                nc.scalar.activation(out=squares[:, j, :], in_=product[:], func=ACT.Square)
+                if j == 0:
+                    copied = copy_pool.tile([P, 2 * N], F32)
+                    nc.vector.tensor_copy(out=copied[:], in_=product[:])
+                    nc.vector.tensor_tensor(
+                        out=squares[:, j, :], in0=product[:], in1=copied[:], op=ALU.mult
+                    )
+                else:
+                    nc.scalar.activation(
+                        out=squares[:, j, :], in_=product[:], func=ACT.Square
+                    )
             square_tiles[g] = squares
 
         def add_squares(g):
             squares = square_tiles[g]
             power = out_pool.tile([P, TILES, N], F32)
-            nc.vector.tensor_tensor(
+            nc.gpsimd.tensor_tensor(
                 out=power[:], in0=squares[:, :, 0:N], in1=squares[:, :, N : 2 * N], op=ALU.add
             )
             out_tiles[g] = power
@@ -148,8 +158,8 @@ def tile_dft_kernel(
         for g in range(1, LOADS_AHEAD):
             load_x(g)
 
-        for step in range(N_GROUPS + 2):
-            turning, projecting, finishing = step, step - 1, step - 2
+        for step in range(N_GROUPS + 3):
+            turning, projecting, adding, finishing = step, step - 1, step - 2, step - 3
             if turning + LOADS_AHEAD < N_GROUPS:
                 load_x(turning + LOADS_AHEAD)
             if turning < N_GROUPS:
@@ -157,8 +167,8 @@ def tile_dft_kernel(
                 regroup(turning)
             if 0 <= projecting < N_GROUPS:
                 project_and_square(projecting)
-            if finishing >= 0:
-                add_squares(finishing)
+            if 0 <= adding < N_GROUPS:
+                add_squares(adding)
             if turning < N_GROUPS:
                 quantise(turning)
             if finishing >= 0:

@@ -21,6 +21,8 @@ TILES = 4
 GROUP_ROWS = TILES * P
 N_GROUPS = ROWS // GROUP_ROWS
 WORDS = K // 2
+VECTOR_TILE = TILES - 1
+SCALAR_COLS = 128
 LOADS_AHEAD = 7
 
 FLOPS = 2 * ROWS * K * 2 * N
@@ -42,20 +44,28 @@ def tile_dft_kernel(
         copy_pool = ctx.enter_context(tc.tile_pool(name="copy", bufs=2))
         squares_pool = ctx.enter_context(tc.tile_pool(name="squares", bufs=3))
         out_pool = ctx.enter_context(tc.tile_pool(name="out", bufs=4))
-        turned_pool = ctx.enter_context(tc.psum_pool(name="turned", bufs=4))
-        product_pool = ctx.enter_context(tc.psum_pool(name="product", bufs=4))
+        turned_pool = ctx.enter_context(tc.psum_pool(name="turned", bufs=3))
+        scalar_banks = ctx.enter_context(tc.psum_pool(name="scalar_banks", bufs=3))
+        vector_banks = ctx.enter_context(tc.psum_pool(name="vector_banks", bufs=2))
 
         x_tiles = {}
         turned_tiles = {}
         grouped_tiles = {}
         code_tiles = {}
         square_tiles = {}
+        vector_products = {}
+        copied_tiles = {}
         out_tiles = {}
 
         def load_x(g):
             x_sb = x_pool.tile([P, TILES, K], BF16)
-            nc.sync.dma_start(out=x_sb[:], in_=x_groups[g])
             x_tiles[g] = x_sb
+            if g == 0:
+                for half in range(2):
+                    tiles = slice(half * TILES // 2, (half + 1) * TILES // 2)
+                    nc.sync.dma_start(out=x_sb[:, tiles, :], in_=x_groups[g][:, tiles, :])
+            else:
+                nc.sync.dma_start(out=x_sb[:], in_=x_groups[g])
 
         def transpose_group(g):
             x_words = x_tiles[g][:].bitcast(F32)
@@ -71,15 +81,15 @@ def tile_dft_kernel(
                         )
                 turned_tiles[g].append(turned)
 
-        def regroup(g):
-            grouped = grouped_pool.tile([P, TILES, P, PACK], BF16, align_bytes=64)
-            grouped_words = grouped[:].bitcast(F32)
-            for half in range(TILES // 2):
-                nc.vector.tensor_copy(
-                    out=grouped_words[:, 2 * half : 2 * half + 2, :, :],
-                    in_=turned_tiles[g][half][:].rearrange("p j u r -> p j r u"),
-                )
-            grouped_tiles[g] = grouped
+        def regroup(g, half):
+            if half == 0:
+                grouped = grouped_pool.tile([P, TILES, P, PACK], BF16, align_bytes=64)
+                grouped_tiles[g] = grouped
+            grouped_words = grouped_tiles[g][:].bitcast(F32)
+            nc.vector.tensor_copy(
+                out=grouped_words[:, 2 * half : 2 * half + 2, :, :],
+                in_=turned_tiles[g][half][:].rearrange("p j u r -> p j r u"),
+            )
 
         def quantise(g):
             x_codes = codes_pool.tile([P, TILES * P], U32, align_bytes=64)
@@ -94,9 +104,14 @@ def tile_dft_kernel(
         def project_and_square(g):
             x_codes, x_scales = code_tiles[g]
             squares = squares_pool.tile([P, TILES, 2 * N], F32)
+            square_tiles[g] = squares
             for j in range(TILES):
                 rows = slice(j * P, (j + 1) * P)
-                product = product_pool.tile([P, 2 * N], F32)
+                if j < VECTOR_TILE:
+                    product = scalar_banks.tile([P, 2 * N], F32)
+                else:
+                    product = vector_banks.tile([P, 2 * N], F32)
+                    vector_products[g] = product
                 nc.tensor.matmul_mx(
                     out=product[:],
                     lhsT=x_codes[:, rows].bitcast(FP8X4),
@@ -106,30 +121,39 @@ def tile_dft_kernel(
                     start=True,
                     stop=True,
                 )
-                if j == 0:
-                    copied = copy_pool.tile([P, 2 * N], F32)
-                    nc.vector.tensor_copy(out=copied[:], in_=product[:])
-                    nc.vector.tensor_tensor(
-                        out=squares[:, j, :], in0=product[:], in1=copied[:], op=ALU.mult
-                    )
-                else:
-                    nc.scalar.activation(
-                        out=squares[:, j, :], in_=product[:], func=ACT.Square
-                    )
-            square_tiles[g] = squares
+                width = 2 * N if j < VECTOR_TILE else SCALAR_COLS
+                nc.scalar.activation(
+                    out=squares[:, j, 0:width], in_=product[:, 0:width], func=ACT.Square
+                )
 
-        def add_squares(g):
-            squares = square_tiles[g]
-            power = out_pool.tile([P, TILES, N], F32)
-            nc.gpsimd.tensor_tensor(
-                out=power[:], in0=squares[:, :, 0:N], in1=squares[:, :, N : 2 * N], op=ALU.add
+        def vector_copy(g):
+            copied = copy_pool.tile([P, 2 * N - SCALAR_COLS], F32)
+            nc.vector.tensor_copy(out=copied[:], in_=vector_products[g][:, SCALAR_COLS:])
+            copied_tiles[g] = copied
+
+        def vector_square(g):
+            nc.vector.tensor_tensor(
+                out=square_tiles[g][:, VECTOR_TILE, SCALAR_COLS:],
+                in0=vector_products[g][:, SCALAR_COLS:],
+                in1=copied_tiles[g][:],
+                op=ALU.mult,
             )
-            out_tiles[g] = power
+
+        def add_squares(g, engine, tiles):
+            squares = square_tiles[g]
+            engine.tensor_tensor(
+                out=out_tiles[g][:, tiles, :],
+                in0=squares[:, tiles, 0:N],
+                in1=squares[:, tiles, N : 2 * N],
+                op=ALU.add,
+            )
 
         def log_and_store(g):
-            power = out_tiles[g]
-            nc.scalar.activation(out=power[:], in_=power[:], func=ACT.Ln)
-            nc.sync.dma_start(out=out_groups[g], in_=power[:])
+            for half in range(2):
+                tiles = slice(half * TILES // 2, (half + 1) * TILES // 2)
+                power = out_tiles[g][:, tiles, :]
+                nc.scalar.activation(out=power, in_=power, func=ACT.Ln)
+                nc.sync.dma_start(out=out_groups[g][:, tiles, :], in_=power)
 
         w_scales = consts.tile([P, 2 * N], U8, align_bytes=64)
         nc.vector.memset(w_scales[:].bitcast(I32), 0)
@@ -141,20 +165,21 @@ def tile_dft_kernel(
 
         load_x(0)
         w_codes = consts.tile([P, 2 * N], U32, align_bytes=64)
-        for m, (words, scales) in enumerate(
-            ((dft_real_words, dft_real_scales), (dft_imag_words, dft_imag_scales))
-        ):
-            cols = slice(m * N, (m + 1) * N)
-            nc.sync.dma_start(
-                out=w_codes[:, cols].bitcast(I32),
-                in_=words.rearrange("g p n t -> (g p) (n t)").bitcast(I32),
-            )
-            scale_rows = scales.rearrange("g q n -> (g q) n")
+        weights = ((dft_real_words, dft_real_scales), (dft_imag_words, dft_imag_scales))
+        for m in range(2):
+            scale_rows = weights[m][1].rearrange("g q n -> (g q) n")
             for quadrant in range(4):
                 nc.sync.dma_start(
-                    out=w_scales[32 * quadrant : 32 * quadrant + 4, cols].bitcast(I32),
+                    out=w_scales[
+                        32 * quadrant : 32 * quadrant + 4, m * N : (m + 1) * N
+                    ].bitcast(I32),
                     in_=scale_rows[4 * quadrant : 4 * quadrant + 4, :].bitcast(I32),
                 )
+        for m in range(2):
+            nc.sync.dma_start(
+                out=w_codes[:, m * N : (m + 1) * N].bitcast(I32),
+                in_=weights[m][0].rearrange("g p n t -> (g p) (n t)").bitcast(I32),
+            )
         for g in range(1, LOADS_AHEAD):
             load_x(g)
 
@@ -164,12 +189,21 @@ def tile_dft_kernel(
                 load_x(turning + LOADS_AHEAD)
             if turning < N_GROUPS:
                 transpose_group(turning)
-                regroup(turning)
+                regroup(turning, 0)
+            if 0 <= adding < N_GROUPS:
+                vector_copy(adding)
+            if turning < N_GROUPS:
+                regroup(turning, 1)
+            if 0 <= adding < N_GROUPS:
+                vector_square(adding)
             if 0 <= projecting < N_GROUPS:
                 project_and_square(projecting)
-            if 0 <= adding < N_GROUPS:
-                add_squares(adding)
             if turning < N_GROUPS:
                 quantise(turning)
+            if 0 <= adding < N_GROUPS:
+                power = out_pool.tile([P, TILES, N], F32)
+                out_tiles[adding] = power
+                add_squares(adding, nc.vector, slice(VECTOR_TILE, TILES))
+                add_squares(adding, nc.gpsimd, slice(0, VECTOR_TILE))
             if finishing >= 0:
                 log_and_store(finishing)

@@ -149,8 +149,9 @@ def tile_dft_kernel(
             )
 
         def log_and_store(g):
-            for half in range(2):
-                tiles = slice(half * TILES // 2, (half + 1) * TILES // 2)
+            pieces = 2 if g == N_GROUPS - 1 else 1
+            for piece in range(pieces):
+                tiles = slice(piece * TILES // pieces, (piece + 1) * TILES // pieces)
                 power = out_tiles[g][:, tiles, :]
                 nc.scalar.activation(out=power, in_=power, func=ACT.Ln)
                 nc.sync.dma_start(out=out_groups[g][:, tiles, :], in_=power)

@@ -24,6 +24,7 @@ WORDS = K // 2
 VECTOR_TILE = TILES - 1
 SCALAR_COLS = 128
 LOADS_AHEAD = 7
+WORK_BUFS = 5
 
 FLOPS = 2 * ROWS * K * 2 * N
 
@@ -39,23 +40,21 @@ def tile_dft_kernel(
         ctx.enter_context(tc.manual_schedule())
         consts = ctx.enter_context(tc.tile_pool(name="consts", bufs=1))
         x_pool = ctx.enter_context(tc.tile_pool(name="x", bufs=LOADS_AHEAD + 1))
-        grouped_pool = ctx.enter_context(tc.tile_pool(name="grouped", bufs=2))
+        work_pool = ctx.enter_context(tc.tile_pool(name="work", bufs=WORK_BUFS))
         codes_pool = ctx.enter_context(tc.tile_pool(name="codes", bufs=2))
         copy_pool = ctx.enter_context(tc.tile_pool(name="copy", bufs=2))
         squares_pool = ctx.enter_context(tc.tile_pool(name="squares", bufs=3))
-        out_pool = ctx.enter_context(tc.tile_pool(name="out", bufs=4))
         turned_pool = ctx.enter_context(tc.psum_pool(name="turned", bufs=3))
         scalar_banks = ctx.enter_context(tc.psum_pool(name="scalar_banks", bufs=3))
         vector_banks = ctx.enter_context(tc.psum_pool(name="vector_banks", bufs=2))
 
         x_tiles = {}
         turned_tiles = {}
-        grouped_tiles = {}
+        work_tiles = {}
         code_tiles = {}
         square_tiles = {}
         vector_products = {}
         copied_tiles = {}
-        out_tiles = {}
 
         def load_x(g):
             x_sb = x_pool.tile([P, TILES, K], BF16)
@@ -82,10 +81,7 @@ def tile_dft_kernel(
                 turned_tiles[g].append(turned)
 
         def regroup(g, half):
-            if half == 0:
-                grouped = grouped_pool.tile([P, TILES, P, PACK], BF16, align_bytes=64)
-                grouped_tiles[g] = grouped
-            grouped_words = grouped_tiles[g][:].bitcast(F32)
+            grouped_words = work_tiles[g][:].rearrange("p j (r u) -> p j r u", u=2)
             nc.vector.tensor_copy(
                 out=grouped_words[:, 2 * half : 2 * half + 2, :, :],
                 in_=turned_tiles[g][half][:].rearrange("p j u r -> p j r u"),
@@ -97,7 +93,7 @@ def tile_dft_kernel(
             nc.vector.quantize_mx(
                 out=x_codes[:].bitcast(FP8X4),
                 scales=x_scales[:],
-                in_=grouped_tiles[g][:].rearrange("p j r t -> p (j r t)"),
+                in_=work_tiles[g][:].rearrange("p j w -> p (j w)").bitcast(BF16),
             )
             code_tiles[g] = (x_codes, x_scales)
 
@@ -142,7 +138,7 @@ def tile_dft_kernel(
         def add_squares(g, engine, tiles):
             squares = square_tiles[g]
             engine.tensor_tensor(
-                out=out_tiles[g][:, tiles, :],
+                out=work_tiles[g + 1][:, tiles, :],
                 in0=squares[:, tiles, 0:N],
                 in1=squares[:, tiles, N : 2 * N],
                 op=ALU.add,
@@ -152,7 +148,7 @@ def tile_dft_kernel(
             pieces = 2 if g == N_GROUPS - 1 else 1
             for piece in range(pieces):
                 tiles = slice(piece * TILES // pieces, (piece + 1) * TILES // pieces)
-                power = out_tiles[g][:, tiles, :]
+                power = work_tiles[g + 1][:, tiles, :]
                 nc.scalar.activation(out=power, in_=power, func=ACT.Ln)
                 nc.sync.dma_start(out=out_groups[g][:, tiles, :], in_=power)
 
@@ -188,6 +184,9 @@ def tile_dft_kernel(
             turning, projecting, adding, finishing = step, step - 1, step - 2, step - 3
             if turning + LOADS_AHEAD < N_GROUPS:
                 load_x(turning + LOADS_AHEAD)
+            if turning <= N_GROUPS:
+                work = work_pool.tile([P, TILES, N], F32, align_bytes=64)
+                work_tiles[turning] = work
             if turning < N_GROUPS:
                 transpose_group(turning)
                 regroup(turning, 0)
@@ -202,9 +201,8 @@ def tile_dft_kernel(
             if turning < N_GROUPS:
                 quantise(turning)
             if 0 <= adding < N_GROUPS:
-                power = out_pool.tile([P, TILES, N], F32)
-                out_tiles[adding] = power
                 add_squares(adding, nc.vector, slice(VECTOR_TILE, TILES))
-                add_squares(adding, nc.gpsimd, slice(0, VECTOR_TILE))
+            if 0 <= projecting < N_GROUPS:
+                add_squares(projecting, nc.gpsimd, slice(0, VECTOR_TILE))
             if finishing >= 0:
                 log_and_store(finishing)

@@ -23,6 +23,7 @@ N_GROUPS = ROWS // GROUP_ROWS
 WORDS = K // 2
 VECTOR_TILE = TILES - 1
 SCALAR_COLS = 128
+SCALAR_ONLY_GROUPS = 2
 LOADS_AHEAD = 7
 WORK_BUFS = 5
 
@@ -42,11 +43,19 @@ def tile_dft_kernel(
         x_pool = ctx.enter_context(tc.tile_pool(name="x", bufs=LOADS_AHEAD + 1))
         work_pool = ctx.enter_context(tc.tile_pool(name="work", bufs=WORK_BUFS))
         codes_pool = ctx.enter_context(tc.tile_pool(name="codes", bufs=2))
-        copy_pool = ctx.enter_context(tc.tile_pool(name="copy", bufs=2))
+        copy_pool = ctx.enter_context(tc.tile_pool(name="copy", bufs=3))
         squares_pool = ctx.enter_context(tc.tile_pool(name="squares", bufs=3))
         turned_pool = ctx.enter_context(tc.psum_pool(name="turned", bufs=3))
         scalar_banks = ctx.enter_context(tc.psum_pool(name="scalar_banks", bufs=3))
         vector_banks = ctx.enter_context(tc.psum_pool(name="vector_banks", bufs=2))
+
+        def first_vector_tile(g):
+            if g < SCALAR_ONLY_GROUPS:
+                return TILES
+            return VECTOR_TILE - 1 if g == N_GROUPS - 1 else VECTOR_TILE
+
+        def scalar_cols(g):
+            return 0 if g >= N_GROUPS - 2 else SCALAR_COLS
 
         x_tiles = {}
         turned_tiles = {}
@@ -87,27 +96,32 @@ def tile_dft_kernel(
                 in_=turned_tiles[g][half][:].rearrange("p j u r -> p j r u"),
             )
 
-        def quantise(g):
-            x_codes = codes_pool.tile([P, TILES * P], U32, align_bytes=64)
-            x_scales = codes_pool.tile([P, TILES * P], U8, align_bytes=64)
-            nc.vector.quantize_mx(
-                out=x_codes[:].bitcast(FP8X4),
-                scales=x_scales[:],
-                in_=work_tiles[g][:].rearrange("p j w -> p (j w)").bitcast(BF16),
-            )
-            code_tiles[g] = (x_codes, x_scales)
-
-        def project_and_square(g):
+        def quantise(g, first, last):
+            if first == 0:
+                x_codes = codes_pool.tile([P, TILES * P], U32, align_bytes=64)
+                x_scales = codes_pool.tile([P, TILES * P], U8, align_bytes=64)
+                code_tiles[g] = (x_codes, x_scales)
             x_codes, x_scales = code_tiles[g]
-            squares = squares_pool.tile([P, TILES, 2 * N], F32)
-            square_tiles[g] = squares
-            for j in range(TILES):
+            rows = slice(first * P, last * P)
+            nc.vector.quantize_mx(
+                out=x_codes[:, rows].bitcast(FP8X4),
+                scales=x_scales[:, rows],
+                in_=work_tiles[g][:, first:last, :].rearrange("p j w -> p (j w)").bitcast(BF16),
+            )
+
+        def project_and_square(g, first, last):
+            x_codes, x_scales = code_tiles[g]
+            if first == 0:
+                squares = squares_pool.tile([P, TILES, 2 * N], F32)
+                square_tiles[g] = squares
+            squares = square_tiles[g]
+            for j in range(first, last):
                 rows = slice(j * P, (j + 1) * P)
-                if j < VECTOR_TILE:
+                if j < min(first_vector_tile(g), VECTOR_TILE):
                     product = scalar_banks.tile([P, 2 * N], F32)
                 else:
                     product = vector_banks.tile([P, 2 * N], F32)
-                    vector_products[g] = product
+                    vector_products[(g, j)] = product
                 nc.tensor.matmul_mx(
                     out=product[:],
                     lhsT=x_codes[:, rows].bitcast(FP8X4),
@@ -117,23 +131,28 @@ def tile_dft_kernel(
                     start=True,
                     stop=True,
                 )
-                width = 2 * N if j < VECTOR_TILE else SCALAR_COLS
-                nc.scalar.activation(
-                    out=squares[:, j, 0:width], in_=product[:, 0:width], func=ACT.Square
-                )
+                width = 2 * N if j < first_vector_tile(g) else scalar_cols(g)
+                if width > 0:
+                    nc.scalar.activation(
+                        out=squares[:, j, 0:width], in_=product[:, 0:width], func=ACT.Square
+                    )
 
         def vector_copy(g):
-            copied = copy_pool.tile([P, 2 * N - SCALAR_COLS], F32)
-            nc.vector.tensor_copy(out=copied[:], in_=vector_products[g][:, SCALAR_COLS:])
-            copied_tiles[g] = copied
+            for j in range(first_vector_tile(g), TILES):
+                copied = copy_pool.tile([P, 2 * N - scalar_cols(g)], F32)
+                nc.vector.tensor_copy(
+                    out=copied[:], in_=vector_products[(g, j)][:, scalar_cols(g) :]
+                )
+                copied_tiles[(g, j)] = copied
 
         def vector_square(g):
-            nc.vector.tensor_tensor(
-                out=square_tiles[g][:, VECTOR_TILE, SCALAR_COLS:],
-                in0=vector_products[g][:, SCALAR_COLS:],
-                in1=copied_tiles[g][:],
-                op=ALU.mult,
-            )
+            for j in range(first_vector_tile(g), TILES):
+                nc.vector.tensor_tensor(
+                    out=square_tiles[g][:, j, scalar_cols(g) :],
+                    in0=vector_products[(g, j)][:, scalar_cols(g) :],
+                    in1=copied_tiles[(g, j)][:],
+                    op=ALU.mult,
+                )
 
         def add_squares(g, engine, tiles):
             squares = square_tiles[g]
@@ -190,6 +209,9 @@ def tile_dft_kernel(
             if turning < N_GROUPS:
                 transpose_group(turning)
                 regroup(turning, 0)
+            if turning == 0:
+                quantise(0, 0, TILES // 2)
+                project_and_square(0, 0, TILES // 2)
             if 0 <= adding < N_GROUPS:
                 vector_copy(adding)
             if turning < N_GROUPS:
@@ -197,12 +219,14 @@ def tile_dft_kernel(
             if 0 <= adding < N_GROUPS:
                 vector_square(adding)
             if 0 <= projecting < N_GROUPS:
-                project_and_square(projecting)
+                project_and_square(projecting, TILES // 2 if projecting == 0 else 0, TILES)
             if turning < N_GROUPS:
-                quantise(turning)
+                quantise(turning, TILES // 2 if turning == 0 else 0, TILES)
             if 0 <= adding < N_GROUPS:
-                add_squares(adding, nc.vector, slice(VECTOR_TILE, TILES))
+                add_squares(adding, nc.vector, slice(min(first_vector_tile(adding), VECTOR_TILE), TILES))
             if 0 <= projecting < N_GROUPS:
-                add_squares(projecting, nc.gpsimd, slice(0, VECTOR_TILE))
+                add_squares(
+                    projecting, nc.gpsimd, slice(0, min(first_vector_tile(projecting), VECTOR_TILE))
+                )
             if finishing >= 0:
                 log_and_store(finishing)

@@ -24,6 +24,7 @@ WORDS = K // 2
 VECTOR_TILE = TILES - 1
 SCALAR_COLS = 128
 SCALAR_ONLY_GROUPS = 2
+PASSES_BEFORE_FIRST_LOAD = 5
 LOADS_AHEAD = 7
 WORK_BUFS = 5
 
@@ -64,6 +65,13 @@ def tile_dft_kernel(
         square_tiles = {}
         vector_products = {}
         copied_tiles = {}
+
+        def warm_up(passes):
+            for i in range(passes):
+                product = scalar_banks.tile([P, 2 * N], F32)
+                nc.tensor.matmul(
+                    out=product[:], lhsT=zeros[:, 0:P], rhs=zeros[:], start=True, stop=True
+                )
 
         def load_x(g):
             x_sb = x_pool.tile([P, TILES, K], BF16)
@@ -171,6 +179,8 @@ def tile_dft_kernel(
                 nc.scalar.activation(out=power, in_=power, func=ACT.Ln)
                 nc.sync.dma_start(out=out_groups[g][:, tiles, :], in_=power)
 
+        zeros = consts.tile([P, 2 * N], BF16)
+        nc.vector.memset(zeros[:], 0.0)
         w_scales = consts.tile([P, 2 * N], U8, align_bytes=64)
         nc.vector.memset(w_scales[:].bitcast(I32), 0)
         one = consts.tile([P, 1], F32)
@@ -179,6 +189,7 @@ def tile_dft_kernel(
         identity = consts.tile([P, P], F32)
         make_identity(nc, identity[:])
 
+        warm_up(PASSES_BEFORE_FIRST_LOAD)
         load_x(0)
         w_codes = consts.tile([P, 2 * N], U32, align_bytes=64)
         weights = ((dft_real_words, dft_real_scales), (dft_imag_words, dft_imag_scales))
@@ -210,6 +221,7 @@ def tile_dft_kernel(
                 transpose_group(turning)
                 regroup(turning, 0)
             if turning == 0:
+                warm_up(1)
                 quantise(0, 0, TILES // 2)
                 project_and_square(0, 0, TILES // 2)
             if 0 <= adding < N_GROUPS:

@@ -44,7 +44,6 @@ def tile_dft_kernel(
         x_pool = ctx.enter_context(tc.tile_pool(name="x", bufs=LOADS_AHEAD + 1))
         work_pool = ctx.enter_context(tc.tile_pool(name="work", bufs=WORK_BUFS))
         codes_pool = ctx.enter_context(tc.tile_pool(name="codes", bufs=2))
-        copy_pool = ctx.enter_context(tc.tile_pool(name="copy", bufs=3))
         squares_pool = ctx.enter_context(tc.tile_pool(name="squares", bufs=3))
         turned_pool = ctx.enter_context(tc.psum_pool(name="turned", bufs=3))
         scalar_banks = ctx.enter_context(tc.psum_pool(name="scalar_banks", bufs=3))
@@ -64,7 +63,6 @@ def tile_dft_kernel(
         code_tiles = {}
         square_tiles = {}
         vector_products = {}
-        copied_tiles = {}
 
         def warm_up(passes):
             for i in range(passes):
@@ -145,20 +143,14 @@ def tile_dft_kernel(
                         out=squares[:, j, 0:width], in_=product[:, 0:width], func=ACT.Square
                     )
 
-        def vector_copy(g):
-            for j in range(first_vector_tile(g), TILES):
-                copied = copy_pool.tile([P, 2 * N - scalar_cols(g)], F32)
-                nc.vector.tensor_copy(
-                    out=copied[:], in_=vector_products[(g, j)][:, scalar_cols(g) :]
-                )
-                copied_tiles[(g, j)] = copied
-
         def vector_square(g):
             for j in range(first_vector_tile(g), TILES):
-                nc.vector.tensor_tensor(
+                width = 2 * N - scalar_cols(g)
+                columns = vector_products[(g, j)][:, scalar_cols(g) :]
+                nc.vector.tensor_reduce(
                     out=square_tiles[g][:, j, scalar_cols(g) :],
-                    in0=vector_products[(g, j)][:, scalar_cols(g) :],
-                    in1=copied_tiles[(g, j)][:],
+                    in_=columns.unsqueeze(2).to_broadcast([P, width, 2]),
+                    axis=mybir.AxisListType.X,
                     op=ALU.mult,
                 )
 
@@ -224,8 +216,6 @@ def tile_dft_kernel(
                 warm_up(1)
                 quantise(0, 0, TILES // 2)
                 project_and_square(0, 0, TILES // 2)
-            if 0 <= adding < N_GROUPS:
-                vector_copy(adding)
             if turning < N_GROUPS:
                 regroup(turning, 1)
             if 0 <= adding < N_GROUPS:

@@ -143,8 +143,8 @@ def tile_dft_kernel(
                         out=squares[:, j, 0:width], in_=product[:, 0:width], func=ACT.Square
                     )
 
-        def vector_square(g):
-            for j in range(first_vector_tile(g), TILES):
+        def vector_square(g, tiles=range(TILES)):
+            for j in [j for j in tiles if j >= first_vector_tile(g)]:
                 width = 2 * N - scalar_cols(g)
                 columns = vector_products[(g, j)][:, scalar_cols(g) :]
                 nc.vector.tensor_reduce(
@@ -164,9 +164,9 @@ def tile_dft_kernel(
             )
 
         def log_and_store(g):
-            pieces = 2 if g == N_GROUPS - 1 else 1
-            for piece in range(pieces):
-                tiles = slice(piece * TILES // pieces, (piece + 1) * TILES // pieces)
+            cuts = [0, 2, 3, 4] if g == N_GROUPS - 1 else [0, 2, 4] if g == N_GROUPS - 2 else [0, 4]
+            for first, end in zip(cuts, cuts[1:]):
+                tiles = slice(first, end)
                 power = work_tiles[g + 1][:, tiles, :]
                 nc.scalar.activation(out=power, in_=power, func=ACT.Ln)
                 nc.sync.dma_start(out=out_groups[g][:, tiles, :], in_=power)
@@ -202,11 +202,11 @@ def tile_dft_kernel(
         for g in range(1, LOADS_AHEAD):
             load_x(g)
 
-        for step in range(N_GROUPS + 3):
+        for step in range(N_GROUPS):
             turning, projecting, adding, finishing = step, step - 1, step - 2, step - 3
             if turning + LOADS_AHEAD < N_GROUPS:
                 load_x(turning + LOADS_AHEAD)
-            if turning <= N_GROUPS:
+            if turning < N_GROUPS:
                 work = work_pool.tile([P, TILES, N], F32, align_bytes=64)
                 work_tiles[turning] = work
             if turning < N_GROUPS:
@@ -232,3 +232,17 @@ def tile_dft_kernel(
                 )
             if finishing >= 0:
                 log_and_store(finishing)
+
+        last = N_GROUPS - 1
+        work = work_pool.tile([P, TILES, N], F32, align_bytes=64)
+        work_tiles[N_GROUPS] = work
+        vector_square(last - 1)
+        log_and_store(last - 2)
+        project_and_square(last, 0, TILES)
+        vector_square(last, [VECTOR_TILE - 1])
+        add_squares(last - 1, nc.vector, slice(VECTOR_TILE, TILES))
+        vector_square(last, [VECTOR_TILE])
+        for half in range(2):
+            add_squares(last, nc.vector, slice(half * TILES // 2, (half + 1) * TILES // 2))
+        for g in (last - 1, last):
+            log_and_store(g)

@@ -24,7 +24,7 @@ WORDS = K // 2
 VECTOR_TILE = TILES - 1
 SCALAR_COLS = 128
 SCALAR_ONLY_GROUPS = 2
-PASSES_BEFORE_FIRST_LOAD = 5
+PASSES_BEFORE_FIRST_LOAD = 2
 LOADS_AHEAD = 7
 WORK_BUFS = 5
 
@@ -71,20 +71,19 @@ def tile_dft_kernel(
                     out=product[:], lhsT=zeros[:, 0:P], rhs=zeros[:], start=True, stop=True
                 )
 
-        def load_x(g):
-            x_sb = x_pool.tile([P, TILES, K], BF16)
-            x_tiles[g] = x_sb
-            if g == 0:
-                for half in range(2):
-                    tiles = slice(half * TILES // 2, (half + 1) * TILES // 2)
-                    nc.sync.dma_start(out=x_sb[:, tiles, :], in_=x_groups[g][:, tiles, :])
-            else:
-                nc.sync.dma_start(out=x_sb[:], in_=x_groups[g])
+        def load_x(g, half=None):
+            if g not in x_tiles:
+                x_sb = x_pool.tile([P, TILES, K], BF16)
+                x_tiles[g] = x_sb
+            tiles = slice(0, TILES) if half is None else slice(half * TILES // 2, (half + 1) * TILES // 2)
+            nc.sync.dma_start(out=x_tiles[g][:, tiles, :], in_=x_groups[g][:, tiles, :])
 
         def transpose_group(g):
             x_words = x_tiles[g][:].bitcast(F32)
             turned_tiles[g] = []
             for half in range(TILES // 2):
+                if (g, half) == (0, 1):
+                    warm_up(1)
                 turned = turned_pool.tile([P, 2, 2, P], F32)
                 for j in range(2):
                     for u in range(2):
@@ -174,7 +173,7 @@ def tile_dft_kernel(
         zeros = consts.tile([P, 2 * N], BF16)
         nc.vector.memset(zeros[:], 0.0)
         w_scales = consts.tile([P, 2 * N], U8, align_bytes=64)
-        nc.vector.memset(w_scales[:].bitcast(I32), 0)
+        nc.gpsimd.memset(w_scales[:].bitcast(I32), 0)
         one = consts.tile([P, 1], F32)
         nc.vector.memset(one[:], 1.0)
         nc.scalar.activation(out=one[:], in_=one[:], func=ACT.Ln)
@@ -182,10 +181,10 @@ def tile_dft_kernel(
         make_identity(nc, identity[:])
 
         warm_up(PASSES_BEFORE_FIRST_LOAD)
-        load_x(0)
         w_codes = consts.tile([P, 2 * N], U32, align_bytes=64)
         weights = ((dft_real_words, dft_real_scales), (dft_imag_words, dft_imag_scales))
-        for m in range(2):
+
+        def load_scales(m):
             scale_rows = weights[m][1].rearrange("g q n -> (g q) n")
             for quadrant in range(4):
                 nc.sync.dma_start(
@@ -194,11 +193,19 @@ def tile_dft_kernel(
                     ].bitcast(I32),
                     in_=scale_rows[4 * quadrant : 4 * quadrant + 4, :].bitcast(I32),
                 )
-        for m in range(2):
+
+        def load_codes(m):
             nc.sync.dma_start(
                 out=w_codes[:, m * N : (m + 1) * N].bitcast(I32),
                 in_=weights[m][0].rearrange("g p n t -> (g p) (n t)").bitcast(I32),
             )
+
+        load_x(0, 0)
+        load_x(0, 1)
+        load_scales(0)
+        load_codes(0)
+        load_codes(1)
+        load_scales(1)
         for g in range(1, LOADS_AHEAD):
             load_x(g)
 

@@ -22,7 +22,8 @@ GROUP_ROWS = TILES * P
 N_GROUPS = ROWS // GROUP_ROWS
 WORDS = K // 2
 VECTOR_TILE = TILES - 1
-SCALAR_COLS = 128
+SCALAR_COLS = 56
+VECTOR_MORE = 32
 SCALAR_ONLY_GROUPS = 2
 PASSES_BEFORE_FIRST_LOAD = 2
 LOADS_AHEAD = 7
@@ -56,6 +57,9 @@ def tile_dft_kernel(
 
         def scalar_cols(g):
             return 0 if g >= N_GROUPS - 2 else SCALAR_COLS
+
+        def gpsimd_cols(g):
+            return min(first_vector_tile(g), VECTOR_TILE) * N - VECTOR_MORE
 
         x_tiles = {}
         turned_tiles = {}
@@ -117,7 +121,7 @@ def tile_dft_kernel(
         def project_and_square(g, first, last):
             x_codes, x_scales = code_tiles[g]
             if first == 0:
-                squares = squares_pool.tile([P, TILES, 2 * N], F32)
+                squares = squares_pool.tile([P, 2, TILES, N], F32)
                 square_tiles[g] = squares
             squares = square_tiles[g]
             for j in range(first, last):
@@ -136,29 +140,31 @@ def tile_dft_kernel(
                     start=True,
                     stop=True,
                 )
-                width = 2 * N if j < first_vector_tile(g) else scalar_cols(g)
+                width = N if j < first_vector_tile(g) else scalar_cols(g)
                 if width > 0:
                     nc.scalar.activation(
-                        out=squares[:, j, 0:width], in_=product[:, 0:width], func=ACT.Square
+                        out=squares[:, :, j, 0:width],
+                        in_=product[:].rearrange("p (h n) -> p h n", h=2)[:, :, 0:width],
+                        func=ACT.Square,
                     )
 
         def vector_square(g, tiles=range(TILES)):
             for j in [j for j in tiles if j >= first_vector_tile(g)]:
-                width = 2 * N - scalar_cols(g)
-                columns = vector_products[(g, j)][:, scalar_cols(g) :]
+                first = scalar_cols(g)
+                halves = vector_products[(g, j)][:].rearrange("p (h n) -> p h n", h=2)
                 nc.vector.tensor_reduce(
-                    out=square_tiles[g][:, j, scalar_cols(g) :],
-                    in_=columns.unsqueeze(2).to_broadcast([P, width, 2]),
+                    out=square_tiles[g][:, :, j, first:],
+                    in_=halves[:, :, first:].unsqueeze(3).to_broadcast([P, 2, N - first, 2]),
                     axis=mybir.AxisListType.X,
                     op=ALU.mult,
                 )
 
-        def add_squares(g, engine, tiles):
-            squares = square_tiles[g]
+        def add_squares(g, engine, first, end):
+            squares = square_tiles[g][:].rearrange("p h j n -> p h (j n)")
             engine.tensor_tensor(
-                out=work_tiles[g + 1][:, tiles, :],
-                in0=squares[:, tiles, 0:N],
-                in1=squares[:, tiles, N : 2 * N],
+                out=work_tiles[g + 1][:].rearrange("p j n -> p (j n)")[:, first:end],
+                in0=squares[:, 0, first:end],
+                in1=squares[:, 1, first:end],
                 op=ALU.add,
             )
 
@@ -232,11 +238,9 @@ def tile_dft_kernel(
             if turning < N_GROUPS:
                 quantise(turning, TILES // 2 if turning == 0 else 0, TILES)
             if 0 <= adding < N_GROUPS:
-                add_squares(adding, nc.vector, slice(min(first_vector_tile(adding), VECTOR_TILE), TILES))
+                add_squares(adding, nc.vector, gpsimd_cols(adding), TILES * N)
             if 0 <= projecting < N_GROUPS:
-                add_squares(
-                    projecting, nc.gpsimd, slice(0, min(first_vector_tile(projecting), VECTOR_TILE))
-                )
+                add_squares(projecting, nc.gpsimd, 0, gpsimd_cols(projecting))
             if finishing >= 0:
                 log_and_store(finishing)
 
@@ -247,9 +251,9 @@ def tile_dft_kernel(
         log_and_store(last - 2)
         project_and_square(last, 0, TILES)
         vector_square(last, [VECTOR_TILE - 1])
-        add_squares(last - 1, nc.vector, slice(VECTOR_TILE, TILES))
+        add_squares(last - 1, nc.vector, gpsimd_cols(last - 1), TILES * N)
         vector_square(last, [VECTOR_TILE])
         for half in range(2):
-            add_squares(last, nc.vector, slice(half * TILES // 2, (half + 1) * TILES // 2))
+            add_squares(last, nc.vector, half * TILES * N // 2, (half + 1) * TILES * N // 2)
         for g in (last - 1, last):
             log_and_store(g)

from contextlib import ExitStack

import concourse.mybir as mybir
from concourse.masks import make_identity

F32 = mybir.dt.float32
BF16 = mybir.dt.bfloat16
I32 = mybir.dt.int32
U32 = mybir.dt.uint32
U8 = mybir.dt.uint8
FP8X4 = mybir.dt.float8_e4m3fn_x4
ACT = mybir.ActivationFunctionType
ALU = mybir.AluOpType

P = 128
PACK = 4
ROWS, K, N = 16384, 512, 256
assert K == P * PACK

TILES = 4
GROUP_ROWS = TILES * P
N_GROUPS = ROWS // GROUP_ROWS
WORDS = K // 2
VECTOR_TILE = TILES - 1
SCALAR_COLS = 56
VECTOR_MORE = 32
SCALAR_ONLY_GROUPS = 2
PASSES_BEFORE_FIRST_LOAD = 2
LOADS_AHEAD = 7
WORK_BUFS = 5

FLOPS = 2 * ROWS * K * 2 * N


def tile_dft_kernel(
    tc, x, dft_real_words, dft_real_scales, dft_imag_words, dft_imag_scales, out
):
    nc = tc.nc
    x_groups = x.rearrange("(g p j) k -> g p j k", p=P, j=TILES)
    out_groups = out.rearrange("(g p j) n -> g p j n", p=P, j=TILES)

    with ExitStack() as ctx:
        ctx.enter_context(tc.manual_schedule())
        consts = ctx.enter_context(tc.tile_pool(name="consts", bufs=1))
        x_pool = ctx.enter_context(tc.tile_pool(name="x", bufs=LOADS_AHEAD + 1))
        work_pool = ctx.enter_context(tc.tile_pool(name="work", bufs=WORK_BUFS))
        codes_pool = ctx.enter_context(tc.tile_pool(name="codes", bufs=2))
        squares_pool = ctx.enter_context(tc.tile_pool(name="squares", bufs=3))
        turned_pool = ctx.enter_context(tc.psum_pool(name="turned", bufs=3))
        scalar_banks = ctx.enter_context(tc.psum_pool(name="scalar_banks", bufs=3))
        vector_banks = ctx.enter_context(tc.psum_pool(name="vector_banks", bufs=2))

        def first_vector_tile(g):
            if g < SCALAR_ONLY_GROUPS:
                return TILES
            return VECTOR_TILE - 1 if g == N_GROUPS - 1 else VECTOR_TILE

        def scalar_cols(g):
            return 0 if g >= N_GROUPS - 2 else SCALAR_COLS

        def gpsimd_cols(g):
            return min(first_vector_tile(g), VECTOR_TILE) * N - VECTOR_MORE

        x_tiles = {}
        turned_tiles = {}
        work_tiles = {}
        code_tiles = {}
        square_tiles = {}
        vector_products = {}

        def warm_up(passes):
            for i in range(passes):
                product = scalar_banks.tile([P, 2 * N], F32)
                nc.tensor.matmul(
                    out=product[:], lhsT=zeros[:, 0:P], rhs=zeros[:], start=True, stop=True
                )

        def load_x(g, half=None):
            if g not in x_tiles:
                x_sb = x_pool.tile([P, TILES, K], BF16)
                x_tiles[g] = x_sb
            tiles = slice(0, TILES) if half is None else slice(half * TILES // 2, (half + 1) * TILES // 2)
            nc.sync.dma_start(out=x_tiles[g][:, tiles, :], in_=x_groups[g][:, tiles, :])

        def transpose_group(g):
            x_words = x_tiles[g][:].bitcast(F32)
            turned_tiles[g] = []
            for half in range(TILES // 2):
                if (g, half) == (0, 1):
                    warm_up(1)
                turned = turned_pool.tile([P, 2, 2, P], F32)
                for j in range(2):
                    for u in range(2):
                        nc.tensor.transpose(
                            out=turned[:, j, u, :],
                            in_=x_words[:, 2 * half + j, u:WORDS:2],
                            identity=identity[:],
                        )
                turned_tiles[g].append(turned)

        def regroup(g, half):
            grouped_words = work_tiles[g][:].rearrange("p j (r u) -> p j r u", u=2)
            nc.vector.tensor_copy(
                out=grouped_words[:, 2 * half : 2 * half + 2, :, :],
                in_=turned_tiles[g][half][:].rearrange("p j u r -> p j r u"),
            )

        def quantise(g, first, last):
            if first == 0:
                x_codes = codes_pool.tile([P, TILES * P], U32, align_bytes=64)
                x_scales = codes_pool.tile([P, TILES * P], U8, align_bytes=64)
                code_tiles[g] = (x_codes, x_scales)
            x_codes, x_scales = code_tiles[g]
            rows = slice(first * P, last * P)
            nc.vector.quantize_mx(
                out=x_codes[:, rows].bitcast(FP8X4),
                scales=x_scales[:, rows],
                in_=work_tiles[g][:, first:last, :].rearrange("p j w -> p (j w)").bitcast(BF16),
            )

        def project_and_square(g, first, last):
            x_codes, x_scales = code_tiles[g]
            if first == 0:
                squares = squares_pool.tile([P, 2, TILES, N], F32)
                square_tiles[g] = squares
            squares = square_tiles[g]
            for j in range(first, last):
                rows = slice(j * P, (j + 1) * P)
                if j < min(first_vector_tile(g), VECTOR_TILE):
                    product = scalar_banks.tile([P, 2 * N], F32)
                else:
                    product = vector_banks.tile([P, 2 * N], F32)
                    vector_products[(g, j)] = product
                nc.tensor.matmul_mx(
                    out=product[:],
                    lhsT=x_codes[:, rows].bitcast(FP8X4),
                    lhsT_scale=x_scales[:, rows],
                    rhs=w_codes[:].bitcast(FP8X4),
                    rhs_scale=w_scales[:],
                    start=True,
                    stop=True,
                )
                width = N if j < first_vector_tile(g) else scalar_cols(g)
                if width > 0:
                    nc.scalar.activation(
                        out=squares[:, :, j, 0:width],
                        in_=product[:].rearrange("p (h n) -> p h n", h=2)[:, :, 0:width],
                        func=ACT.Square,
                    )

        def vector_square(g, tiles=range(TILES)):
            for j in [j for j in tiles if j >= first_vector_tile(g)]:
                first = scalar_cols(g)
                halves = vector_products[(g, j)][:].rearrange("p (h n) -> p h n", h=2)
                nc.vector.tensor_reduce(
                    out=square_tiles[g][:, :, j, first:],
                    in_=halves[:, :, first:].unsqueeze(3).to_broadcast([P, 2, N - first, 2]),
                    axis=mybir.AxisListType.X,
                    op=ALU.mult,
                )

        def add_squares(g, engine, first, end):
            squares = square_tiles[g][:].rearrange("p h j n -> p h (j n)")
            engine.tensor_tensor(
                out=work_tiles[g + 1][:].rearrange("p j n -> p (j n)")[:, first:end],
                in0=squares[:, 0, first:end],
                in1=squares[:, 1, first:end],
                op=ALU.add,
            )

        def log_and_store(g):
            cuts = [0, 2, 3, 4] if g == N_GROUPS - 1 else [0, 2, 4] if g == N_GROUPS - 2 else [0, 4]
            for first, end in zip(cuts, cuts[1:]):
                tiles = slice(first, end)
                power = work_tiles[g + 1][:, tiles, :]
                nc.scalar.activation(out=power, in_=power, func=ACT.Ln)
                nc.sync.dma_start(out=out_groups[g][:, tiles, :], in_=power)

        zeros = consts.tile([P, 2 * N], BF16)
        nc.vector.memset(zeros[:], 0.0)
        w_scales = consts.tile([P, 2 * N], U8, align_bytes=64)
        nc.gpsimd.memset(w_scales[:].bitcast(I32), 0)
        one = consts.tile([P, 1], F32)
        nc.vector.memset(one[:], 1.0)
        nc.scalar.activation(out=one[:], in_=one[:], func=ACT.Ln)
        identity = consts.tile([P, P], F32)
        make_identity(nc, identity[:])

        warm_up(PASSES_BEFORE_FIRST_LOAD)
        w_codes = consts.tile([P, 2 * N], U32, align_bytes=64)
        weights = ((dft_real_words, dft_real_scales), (dft_imag_words, dft_imag_scales))

        def load_scales(m):
            scale_rows = weights[m][1].rearrange("g q n -> (g q) n")
            for quadrant in range(4):
                nc.sync.dma_start(
                    out=w_scales[
                        32 * quadrant : 32 * quadrant + 4, m * N : (m + 1) * N
                    ].bitcast(I32),
                    in_=scale_rows[4 * quadrant : 4 * quadrant + 4, :].bitcast(I32),
                )

        def load_codes(m):
            nc.sync.dma_start(
                out=w_codes[:, m * N : (m + 1) * N].bitcast(I32),
                in_=weights[m][0].rearrange("g p n t -> (g p) (n t)").bitcast(I32),
            )

        load_x(0, 0)
        load_x(0, 1)
        load_scales(0)
        load_codes(0)
        load_codes(1)
        load_scales(1)
        for g in range(1, LOADS_AHEAD):
            load_x(g)

        for step in range(N_GROUPS):
            turning, projecting, adding, finishing = step, step - 1, step - 2, step - 3
            if turning + LOADS_AHEAD < N_GROUPS:
                load_x(turning + LOADS_AHEAD)
            if turning < N_GROUPS:
                work = work_pool.tile([P, TILES, N], F32, align_bytes=64)
                work_tiles[turning] = work
            if turning < N_GROUPS:
                transpose_group(turning)
                regroup(turning, 0)
            if turning == 0:
                warm_up(1)
                quantise(0, 0, TILES // 2)
                project_and_square(0, 0, TILES // 2)
            if turning < N_GROUPS:
                regroup(turning, 1)
            if 0 <= adding < N_GROUPS:
                vector_square(adding)
            if 0 <= projecting < N_GROUPS:
                project_and_square(projecting, TILES // 2 if projecting == 0 else 0, TILES)
            if turning < N_GROUPS:
                quantise(turning, TILES // 2 if turning == 0 else 0, TILES)
            if 0 <= adding < N_GROUPS:
                add_squares(adding, nc.vector, gpsimd_cols(adding), TILES * N)
            if 0 <= projecting < N_GROUPS:
                add_squares(projecting, nc.gpsimd, 0, gpsimd_cols(projecting))
            if finishing >= 0:
                log_and_store(finishing)

        last = N_GROUPS - 1
        work = work_pool.tile([P, TILES, N], F32, align_bytes=64)
        work_tiles[N_GROUPS] = work
        vector_square(last - 1)
        log_and_store(last - 2)
        project_and_square(last, 0, TILES)
        vector_square(last, [VECTOR_TILE - 1])
        add_squares(last - 1, nc.vector, gpsimd_cols(last - 1), TILES * N)
        vector_square(last, [VECTOR_TILE])
        for half in range(2):
            add_squares(last, nc.vector, half * TILES * N // 2, (half + 1) * TILES * N // 2)
        for g in (last - 1, last):
            log_and_store(g)
